import numpy as np
import ml_dtypes


def mxq(x, axis, fmt="e4m3"):
    dtype, down = {"e4m3": (ml_dtypes.float8_e4m3fn, 7), "e5m2": (ml_dtypes.float8_e5m2, 14)}[fmt]
    v = np.moveaxis(np.asarray(x, np.float32).astype(ml_dtypes.bfloat16).astype(np.float64), axis, -1)
    blocks = v.reshape(v.shape[:-1] + (-1, 32))
    amax = np.abs(blocks).max(-1, keepdims=True)
    byte = np.maximum(np.where(amax > 0, np.frexp(amax)[1] - 1 + 127, 0) - down, 1)
    scale = np.exp2(byte - 127.0)
    codes = (blocks / scale).astype(np.float32).astype(dtype).astype(np.float64)
    return np.moveaxis((codes * scale).reshape(v.shape), -1, axis)


WIDE = False


def mx_kscale(k):
    if not WIDE:
        return np.ones(k)
    levels = np.array([10, -10, 5, -5, 0])
    a = np.random.permutation(np.resize(levels, k // 512 * 4)).reshape(k // 512, 4)
    idx = np.arange(k)
    return np.exp2(a[idx // 512, idx % 128 // 32])


BF16 = ml_dtypes.bfloat16


def bf(x):
    return np.asarray(x, np.float32).astype(BF16)


def f64(x):
    return np.asarray(x).astype(np.float64)


E2M1 = np.array([0.0, 0.5, 1.0, 1.5, 2.0, 3.0, 4.0, 6.0, -0.0, -0.5, -1.0, -1.5, -2.0, -3.0, -4.0, -6.0])


def pack_weight(w, fmt):
    k, n = w.shape
    w = f64(bf(w)).reshape(k // 32, 32, n)
    amax = np.abs(w).max(1)
    if fmt == "e4m3":
        byte = np.frexp(amax)[1] - 1 + 127 - 7
    else:
        mant, ex = np.frexp(amax / 6.0)
        byte = np.where(mant > 0.5, ex, ex - 1) + 127
    byte = np.clip(np.where(amax > 0, byte, 1), 1, 254)
    scaled = (w * np.exp2(127.0 - byte)[:, None, :]).reshape(k, n).astype(np.float32)
    by_word = np.ascontiguousarray(scaled.reshape(k // 512, 128, 4, n).transpose(0, 1, 3, 2))
    if fmt == "e4m3":
        words = by_word.astype(ml_dtypes.float8_e4m3fn).view(np.uint8)
    else:
        c = by_word.astype(ml_dtypes.float4_e2m1fn).view(np.uint8) & 0xF
        words = c[..., 0::2] | (c[..., 1::2] << 4)
    return np.ascontiguousarray(words), np.ascontiguousarray(byte.astype(np.uint8).reshape(k // 512, 16, n))


def unpack_weight(words, scales, fmt):
    g, p, n, _ = words.shape
    if fmt == "e4m3":
        vals = np.ascontiguousarray(words).view(ml_dtypes.float8_e4m3fn).astype(np.float64)
    else:
        nib = np.empty((g, p, n, 4), np.uint8)
        nib[..., 0::2] = words & 0xF
        nib[..., 1::2] = words >> 4
        vals = E2M1[nib]
    vals = vals * np.repeat(np.exp2(scales.astype(np.float64) - 127.0), 8, axis=1)[..., None]
    return vals.transpose(0, 1, 3, 2).reshape(g * 512, n)

def pack4(w):
    words, scales = pack_weight(w, "e2m1")
    return words.reshape(words.shape[0], 128, -1), scales


def unpack4(words, scales):
    return unpack_weight(words.reshape(words.shape[0], 128, -1, 2), scales, "e2m1")


B, IN, H = 256, 16384, 1024


def sigmoid(v):
    return 1.0 / (1.0 + np.exp(-v))


def setup_inputs():
    s = mx_kscale(IN)
    inp = bf(np.random.standard_normal((B, IN)) * s)
    state = bf(np.random.standard_normal((B, H)))
    c = bf(np.tanh(np.random.standard_normal((B, H))))
    W2_words, W2_scales = pack4(np.random.standard_normal((IN, H)) * 0.7 / np.sqrt(IN) / s[:, None])
    U2_words, U2_scales = pack4(np.random.standard_normal((H, H)) * 0.7 / np.sqrt(H))
    bias_gate = bf(np.random.standard_normal((1, H)) * 0.5)
    return {'input': inp,
            'state': state,
            'c': c,
            'W2_words': W2_words,
            'W2_scales': W2_scales,
            'U2_words': U2_words,
            'U2_scales': U2_scales,
            'bias_gate': bias_gate}


def reference(input, state, c, W2_words, W2_scales, U2_words, U2_scales, bias_gate):
    h = f64(state)
    wComp2 = mxq(f64(input), 1, 'e4m3') @ unpack4(W2_words, W2_scales)
    uComp2 = mxq(h, 1, 'e4m3') @ unpack4(U2_words, U2_scales)
    z = sigmoid(wComp2 + uComp2 + f64(bias_gate))
    return z * h + (1.0 - z) * f64(c)

@@ -1,0 +1,248 @@
+from contextlib import ExitStack
+
+import concourse.mybir as mybir
+from concourse.masks import make_identity
+
+BF16 = mybir.dt.bfloat16
+F32 = mybir.dt.float32
+I32 = mybir.dt.int32
+U32 = mybir.dt.uint32
+U8 = mybir.dt.uint8
+FP8X4 = mybir.dt.float8_e4m3fn_x4
+FP4X4 = mybir.dt.float4_e2m1fn_x4
+ALU = mybir.AluOpType
+
+P = 128
+PACK = 4
+K_PASS = P * PACK
+ROWS = 256
+K_INPUT = 16384
+HIDDEN = 1024
+ROW_TILES = ROWS // P
+N_PASS = 512
+COL_TILES = HIDDEN // N_PASS
+HALVES = 2
+CHUNK_GROUPS = 4
+QUANT_GROUPS = 2
+SCALE_ROWS = K_PASS // 32
+
+FLOPS = 2 * ROWS * (K_INPUT + HIDDEN) * HIDDEN
+
+
+def tile_grulrcell_pb_k_kernel(
+    tc, inp, state, cand, w2_words, w2_scales, u2_words, u2_scales, bias_gate, out
+):
+    nc = tc.nc
+
+    chunks = [dict(rows=state, words=u2_words, scales=u2_scales, first=0, groups=HIDDEN // K_PASS)]
+    for first in range(0, K_INPUT // K_PASS, CHUNK_GROUPS):
+        chunks.append(
+            dict(rows=inp, words=w2_words, scales=w2_scales, first=first, groups=CHUNK_GROUPS)
+        )
+    n_chunks = len(chunks)
+    total_groups = 0
+    for chunk in chunks:
+        chunk["plane"] = total_groups
+        total_groups += chunk["groups"]
+
+    with ExitStack() as ctx:
+        const = ctx.enter_context(tc.tile_pool(name="const", bufs=1))
+        raw_pool = ctx.enter_context(tc.tile_pool(name="raw", bufs=3))
+        sorted_pool = ctx.enter_context(tc.tile_pool(name="sorted", bufs=2))
+        grouped_pool = ctx.enter_context(tc.tile_pool(name="grouped", bufs=2))
+        codes_pool = ctx.enter_context(tc.tile_pool(name="codes", bufs=3))
+        w_pool = ctx.enter_context(tc.tile_pool(name="weights", bufs=4))
+        work = ctx.enter_context(tc.tile_pool(name="work", bufs=4))
+        acc_pool = ctx.enter_context(tc.psum_pool(name="acc", bufs=1))
+        xt_pool = ctx.enter_context(tc.psum_pool(name="xt", bufs=CHUNK_GROUPS))
+        ctx.enter_context(tc.manual_schedule())
+
+        ident = const.tile([P, P], F32)
+        ones = const.tile([P, P], BF16)
+        bias_rows = const.tile([P, HIDDEN], BF16)
+        bias_all = const.tile([P, HIDDEN], F32)
+        table_warm = const.tile([P, 1], F32)
+        state_sb = const.tile([P, ROW_TILES * HIDDEN], BF16)
+        cand_sb = const.tile([P, ROW_TILES * HIDDEN], BF16)
+        diff = const.tile([P, ROW_TILES * HIDDEN], F32)
+        w_planes = const.tile([P, total_groups, HIDDEN], U8, align_bytes=64)
+        acc = {}
+        for m in range(ROW_TILES):
+            for h in range(COL_TILES):
+                acc[(m, h)] = acc_pool.tile([P, N_PASS], F32, name="acc_%d_%d" % (m, h))
+
+        raw, words_of, sorted_of, banks_of, grouped_of, codes_of, scales_of = {}, {}, {}, {}, {}, {}, {}
+
+        def load_rows(c):
+            chunk = chunks[c]
+            k_cols = slice(chunk["first"] * K_PASS, (chunk["first"] + chunk["groups"]) * K_PASS)
+            if c == 0:
+                x_raw = state_sb
+            else:
+                x_raw = raw_pool.tile([P, ROW_TILES * chunk["groups"] * K_PASS], BF16)
+            nc.sync.dma_start(
+                out=x_raw[:].rearrange("p (m k) -> p m k", m=ROW_TILES),
+                in_=chunk["rows"].rearrange("(m p) k -> p m k", p=P)[:, :, k_cols],
+            )
+            raw[c] = x_raw
+
+        def zero_planes(c):
+            chunk = chunks[c]
+            planes = w_planes[:, chunk["plane"] : chunk["plane"] + chunk["groups"], :]
+            nc.vector.memset(planes.bitcast(I32), 0)
+
+        def load_weights(c):
+            chunk = chunks[c]
+            groups = slice(chunk["first"], chunk["first"] + chunk["groups"])
+            planes = slice(chunk["plane"], chunk["plane"] + chunk["groups"])
+            for q in range(SCALE_ROWS // 2):
+                partition = 32 * (q // 4) + q % 4
+                nc.sync.dma_start(
+                    out=w_planes[partition : P : 64, planes, :].bitcast(I32),
+                    in_=chunk["scales"]
+                    .bitcast(I32)[groups, q : SCALE_ROWS : SCALE_ROWS // 2, :]
+                    .rearrange("g q n -> q g n"),
+                )
+            w_words = w_pool.tile([P, chunk["groups"], 2 * HIDDEN], U8, align_bytes=64)
+            nc.sync.dma_start(
+                out=w_words[:].bitcast(I32),
+                in_=chunk["words"].bitcast(I32)[groups].rearrange("g p b -> p g b"),
+            )
+            words_of[c] = w_words
+
+        def sort_words(c):
+            x_sorted = sorted_pool.tile([P, ROW_TILES * chunks[c]["groups"], HALVES, P], F32)
+            nc.vector.tensor_copy(
+                out=x_sorted[:],
+                in_=raw[c][:].bitcast(F32).rearrange("r (a p u) -> r a u p", p=P, u=HALVES),
+            )
+            sorted_of[c] = x_sorted
+
+        def transpose(c):
+            n_groups = chunks[c]["groups"]
+            banks_of[c] = []
+            for g in range(n_groups):
+                xt = xt_pool.tile([P, ROW_TILES, HALVES, P], F32, tag="xt")
+                for m in range(ROW_TILES):
+                    for u in range(HALVES):
+                        nc.tensor.transpose(
+                            out=xt[:, m, u, :],
+                            in_=sorted_of[c][:, m * n_groups + g, u, :],
+                            identity=ident[:],
+                        )
+                banks_of[c].append(xt)
+
+        def regroup(c):
+            n_groups = chunks[c]["groups"]
+            grouped = grouped_pool.tile([P, n_groups, ROWS * PACK], BF16, align_bytes=64)
+            for g in range(n_groups):
+                nc.scalar.copy(
+                    out=grouped[:, g, :]
+                    .bitcast(F32)
+                    .rearrange("p (m r u) -> p m r u", m=ROW_TILES, u=HALVES),
+                    in_=banks_of[c][g][:].rearrange("p m u r -> p m r u"),
+                )
+            grouped_of[c] = grouped
+
+        def quantise(c):
+            n_groups = chunks[c]["groups"]
+            x_codes = codes_pool.tile([P, n_groups, ROWS], U32, align_bytes=64)
+            x_scales = codes_pool.tile([P, n_groups, ROWS], U8, align_bytes=64)
+            for g in range(0, n_groups, QUANT_GROUPS):
+                pair = slice(g, g + QUANT_GROUPS)
+                nc.vector.quantize_mx(
+                    out=x_codes[:, pair, :].rearrange("p g r -> p (g r)").bitcast(FP8X4),
+                    scales=x_scales[:, pair, :].rearrange("p g r -> p (g r)"),
+                    in_=grouped_of[c][:, pair, :].rearrange("p g f -> p (g f)"),
+                )
+            codes_of[c] = x_codes
+            scales_of[c] = x_scales
+
+        def multiply(c):
+            chunk = chunks[c]
+            for h in range(COL_TILES):
+                for m in range(ROW_TILES):
+                    for g in range(chunk["groups"]):
+                        plane = chunk["plane"] + g
+                        nc.tensor.matmul_mx(
+                            out=acc[(m, h)][:],
+                            lhsT=codes_of[c][:, g, m * P : (m + 1) * P].bitcast(FP8X4),
+                            lhsT_scale=scales_of[c][:, g, m * P : (m + 1) * P],
+                            rhs=words_of[c][:, g, h * 2 * N_PASS : (h + 1) * 2 * N_PASS].bitcast(FP4X4),
+                            rhs_scale=w_planes[:, plane, h * N_PASS : (h + 1) * N_PASS],
+                            start=(plane == 0),
+                            stop=(plane == total_groups - 1),
+                        )
+
+        def spread_bias():
+            for h in range(COL_TILES):
+                cols = slice(h * N_PASS, (h + 1) * N_PASS)
+                spread = xt_pool.tile([P, N_PASS], F32, tag="xt")
+                nc.tensor.matmul(out=spread[:], lhsT=ones[:], rhs=bias_rows[:, cols], start=True, stop=True)
+                nc.scalar.copy(out=bias_all[:, cols], in_=spread[:])
+
+        load_rows(0)
+        load_rows(1)
+        nc.vector.memset(bias_rows[:], 0.0)
+        nc.vector.memset(ones[:], 1.0)
+        nc.scalar.dma_start(out=bias_rows[0:1, :], in_=bias_gate)
+        nc.scalar.activation(
+            out=table_warm[:], in_=ones[:, 0:1], func=mybir.ActivationFunctionType.Sigmoid
+        )
+        make_identity(nc, ident[:])
+        for c in range(3):
+            zero_planes(c)
+
+        sort_words(0)
+        transpose(0)
+        regroup(0)
+        spread_bias()
+        sort_words(1)
+
+        for c in range(n_chunks):
+            load_weights(c)
+            if c + 2 < n_chunks:
+                load_rows(c + 2)
+            if c + 1 < n_chunks:
+                transpose(c + 1)
+            quantise(c)
+            if c + 2 < n_chunks:
+                sort_words(c + 2)
+            if c + 3 < n_chunks:
+                zero_planes(c + 3)
+            multiply(c)
+            if c + 1 < n_chunks:
+                regroup(c + 1)
+
+        nc.sync.dma_start(
+            out=cand_sb[:].rearrange("p (m n) -> p m n", m=ROW_TILES),
+            in_=cand.rearrange("(m p) n -> p m n", p=P),
+        )
+        nc.vector.tensor_tensor(out=diff[:], in0=state_sb[:], in1=cand_sb[:], op=ALU.subtract)
+
+        sums = [(m, h) for h in range(COL_TILES) for m in range(ROW_TILES)]
+        gates = {}
+
+        def gate(m, h):
+            z = work.tile([P, N_PASS], F32, name="z")
+            nc.vector.tensor_tensor(
+                out=z[:], in0=acc[(m, h)][:], in1=bias_all[:, h * N_PASS : (h + 1) * N_PASS], op=ALU.add
+            )
+            nc.scalar.activation(out=z[:], in_=z[:], func=mybir.ActivationFunctionType.Sigmoid)
+            gates[(m, h)] = z
+
+        def blend(m, h):
+            cols = slice(m * HIDDEN + h * N_PASS, m * HIDDEN + (h + 1) * N_PASS)
+            z = gates[(m, h)]
+            result = work.tile([P, N_PASS], F32, name="result")
+            nc.vector.tensor_tensor(out=z[:], in0=z[:], in1=diff[:, cols], op=ALU.mult)
+            nc.vector.tensor_tensor(out=result[:], in0=z[:], in1=cand_sb[:, cols], op=ALU.add)
+            nc.sync.dma_start(
+                out=out[m * P : (m + 1) * P, h * N_PASS : (h + 1) * N_PASS], in_=result[:]
+            )
+
+        gate(*sums[0])
+        for i in range(1, len(sums)):
+            gate(*sums[i])
+            blend(*sums[i - 1])
+        blend(*sums[-1])

@@ -65,13 +65,12 @@ def tile_grulrcell_pb_k_kernel(
         state_sb = const.tile([P, ROW_TILES * HIDDEN], BF16)
         cand_sb = const.tile([P, ROW_TILES * HIDDEN], BF16)
         diff = const.tile([P, ROW_TILES * HIDDEN], F32)
-        w_planes = const.tile([P, total_groups, HIDDEN], U8, align_bytes=64)
         acc = {}
         for m in range(ROW_TILES):
             for h in range(COL_TILES):
                 acc[(m, h)] = acc_pool.tile([P, N_PASS], F32, name="acc_%d_%d" % (m, h))
 
-        raw, words_of, sorted_of, banks_of, grouped_of, codes_of, scales_of = {}, {}, {}, {}, {}, {}, {}
+        raw, words_of, planes_of, sorted_of, banks_of, grouped_of, codes_of, scales_of = {}, {}, {}, {}, {}, {}, {}, {}
 
         def load_rows(c):
             chunk = chunks[c]
@@ -87,18 +86,17 @@ def tile_grulrcell_pb_k_kernel(
             raw[c] = x_raw
 
         def zero_planes(c):
-            chunk = chunks[c]
-            planes = w_planes[:, chunk["plane"] : chunk["plane"] + chunk["groups"], :]
-            nc.vector.memset(planes.bitcast(I32), 0)
+            w_planes = const.tile([P, chunks[c]["groups"], HIDDEN], U8, align_bytes=64, name="w_planes_%d" % c)
+            nc.vector.memset(w_planes[:].bitcast(I32), 0)
+            planes_of[c] = w_planes
 
         def load_weights(c):
             chunk = chunks[c]
             groups = slice(chunk["first"], chunk["first"] + chunk["groups"])
-            planes = slice(chunk["plane"], chunk["plane"] + chunk["groups"])
             for q in range(SCALE_ROWS // 2):
                 partition = 32 * (q // 4) + q % 4
                 nc.sync.dma_start(
-                    out=w_planes[partition : P : 64, planes, :].bitcast(I32),
+                    out=planes_of[c][partition : P : 64, :, :].bitcast(I32),
                     in_=chunk["scales"]
                     .bitcast(I32)[groups, q : SCALE_ROWS : SCALE_ROWS // 2, :]
                     .rearrange("g q n -> q g n"),
@@ -169,7 +167,7 @@ def tile_grulrcell_pb_k_kernel(
                             lhsT=codes_of[c][:, g, m * P : (m + 1) * P].bitcast(FP8X4),
                             lhsT_scale=scales_of[c][:, g, m * P : (m + 1) * P],
                             rhs=words_of[c][:, g, h * 2 * N_PASS : (h + 1) * 2 * N_PASS].bitcast(FP4X4),
-                            rhs_scale=w_planes[:, plane, h * N_PASS : (h + 1) * N_PASS],
+                            rhs_scale=planes_of[c][:, g, h * N_PASS : (h + 1) * N_PASS],
                             start=(plane == 0),
                             stop=(plane == total_groups - 1),
                         )

@@ -93,12 +93,11 @@ def tile_grulrcell_pb_k_kernel(
         def load_weights(c):
             chunk = chunks[c]
             groups = slice(chunk["first"], chunk["first"] + chunk["groups"])
-            for q in range(SCALE_ROWS // 2):
-                partition = 32 * (q // 4) + q % 4
+            for r in range(4):
                 nc.sync.dma_start(
-                    out=planes_of[c][partition : P : 64, :, :].bitcast(I32),
+                    out=planes_of[c][r : P : 32, :, :].bitcast(I32),
                     in_=chunk["scales"]
-                    .bitcast(I32)[groups, q : SCALE_ROWS : SCALE_ROWS // 2, :]
+                    .bitcast(I32)[groups, r : SCALE_ROWS : 4, :]
                     .rearrange("g q n -> q g n"),
                 )
             w_words = w_pool.tile([P, chunk["groups"], 2 * HIDDEN], U8, align_bytes=64)

@@ -25,6 +25,7 @@ HALVES = 2
 CHUNK_GROUPS = 4
 QUANT_GROUPS = 2
 SCALE_ROWS = K_PASS // 32
+SET_CHUNKS = 2
 
 FLOPS = 2 * ROWS * (K_INPUT + HIDDEN) * HIDDEN
 
@@ -34,16 +35,23 @@ def tile_grulrcell_pb_k_kernel(
 ):
     nc = tc.nc
 
-    chunks = [dict(rows=state, words=u2_words, scales=u2_scales, first=0, groups=HIDDEN // K_PASS)]
+    chunks = [dict(rows=state, words=u2_words, first=0, groups=HIDDEN // K_PASS)]
     for first in range(0, K_INPUT // K_PASS, CHUNK_GROUPS):
-        chunks.append(
-            dict(rows=inp, words=w2_words, scales=w2_scales, first=first, groups=CHUNK_GROUPS)
-        )
+        chunks.append(dict(rows=inp, words=w2_words, first=first, groups=CHUNK_GROUPS))
     n_chunks = len(chunks)
     total_groups = 0
     for chunk in chunks:
         chunk["plane"] = total_groups
         total_groups += chunk["groups"]
+    set_groups = SET_CHUNKS * CHUNK_GROUPS
+    sets = [dict(scales=u2_scales, first=0, groups=HIDDEN // K_PASS)]
+    for first in range(0, K_INPUT // K_PASS, set_groups):
+        sets.append(dict(scales=w2_scales, first=first, groups=set_groups))
+    chunks[0]["set"] = 0
+    chunks[0]["in_set"] = 0
+    for c in range(1, n_chunks):
+        chunks[c]["set"] = 1 + (c - 1) // SET_CHUNKS
+        chunks[c]["in_set"] = ((c - 1) % SET_CHUNKS) * CHUNK_GROUPS
 
     with ExitStack() as ctx:
         const = ctx.enter_context(tc.tile_pool(name="const", bufs=1))
@@ -85,21 +93,24 @@ def tile_grulrcell_pb_k_kernel(
             )
             raw[c] = x_raw
 
-        def zero_planes(c):
-            w_planes = const.tile([P, chunks[c]["groups"], HIDDEN], U8, align_bytes=64, name="w_planes_%d" % c)
+        def zero_planes(s):
+            w_planes = const.tile([P, sets[s]["groups"], HIDDEN], U8, align_bytes=64, name="w_planes_%d" % s)
             nc.vector.memset(w_planes[:].bitcast(I32), 0)
-            planes_of[c] = w_planes
+            planes_of[s] = w_planes
 
-        def load_weights(c):
-            chunk = chunks[c]
-            groups = slice(chunk["first"], chunk["first"] + chunk["groups"])
-            for r in range(4):
+        def load_scale_rows(s, rows, apart):
+            groups = slice(sets[s]["first"], sets[s]["first"] + sets[s]["groups"])
+            for q in rows:
                 nc.sync.dma_start(
-                    out=planes_of[c][r : P : 32, :, :].bitcast(I32),
-                    in_=chunk["scales"]
-                    .bitcast(I32)[groups, r : SCALE_ROWS : 4, :]
+                    out=planes_of[s][32 * (q // 4) + q % 4 : P : apart, :, :].bitcast(I32),
+                    in_=sets[s]["scales"]
+                    .bitcast(I32)[groups, q : SCALE_ROWS : apart // 8, :]
                     .rearrange("g q n -> q g n"),
                 )
+
+        def load_words(c):
+            chunk = chunks[c]
+            groups = slice(chunk["first"], chunk["first"] + chunk["groups"])
             w_words = w_pool.tile([P, chunk["groups"], 2 * HIDDEN], U8, align_bytes=64)
             nc.sync.dma_start(
                 out=w_words[:].bitcast(I32),
@@ -166,7 +177,9 @@ def tile_grulrcell_pb_k_kernel(
                             lhsT=codes_of[c][:, g, m * P : (m + 1) * P].bitcast(FP8X4),
                             lhsT_scale=scales_of[c][:, g, m * P : (m + 1) * P],
                             rhs=words_of[c][:, g, h * 2 * N_PASS : (h + 1) * 2 * N_PASS].bitcast(FP4X4),
-                            rhs_scale=planes_of[c][:, g, h * N_PASS : (h + 1) * N_PASS],
+                            rhs_scale=planes_of[chunk["set"]][
+                                :, chunk["in_set"] + g, h * N_PASS : (h + 1) * N_PASS
+                            ],
                             start=(plane == 0),
                             stop=(plane == total_groups - 1),
                         )
@@ -178,17 +191,18 @@ def tile_grulrcell_pb_k_kernel(
                 nc.tensor.matmul(out=spread[:], lhsT=ones[:], rhs=bias_rows[:, cols], start=True, stop=True)
                 nc.scalar.copy(out=bias_all[:, cols], in_=spread[:])
 
-        load_rows(0)
-        load_rows(1)
         nc.vector.memset(bias_rows[:], 0.0)
         nc.vector.memset(ones[:], 1.0)
+        for s in range(len(sets)):
+            zero_planes(s)
+        load_rows(0)
+        load_scale_rows(0, range(4), 32)
+        load_rows(1)
         nc.scalar.dma_start(out=bias_rows[0:1, :], in_=bias_gate)
         nc.scalar.activation(
             out=table_warm[:], in_=ones[:, 0:1], func=mybir.ActivationFunctionType.Sigmoid
         )
         make_identity(nc, ident[:])
-        for c in range(3):
-            zero_planes(c)
 
         sort_words(0)
         transpose(0)
@@ -196,8 +210,16 @@ def tile_grulrcell_pb_k_kernel(
         spread_bias()
         sort_words(1)
 
+        half_rows = SCALE_ROWS // 4
         for c in range(n_chunks):
-            load_weights(c)
+            if 1 + c // 2 < len(sets):
+                load_scale_rows(1 + c // 2, range((c % 2) * half_rows, (c % 2 + 1) * half_rows), 64)
+            if c == n_chunks - 1:
+                nc.sync.dma_start(
+                    out=cand_sb[:].rearrange("p (m n) -> p m n", m=ROW_TILES),
+                    in_=cand.rearrange("(m p) n -> p m n", p=P),
+                )
+            load_words(c)
             if c + 2 < n_chunks:
                 load_rows(c + 2)
             if c + 1 < n_chunks:
@@ -205,16 +227,10 @@ def tile_grulrcell_pb_k_kernel(
             quantise(c)
             if c + 2 < n_chunks:
                 sort_words(c + 2)
-            if c + 3 < n_chunks:
-                zero_planes(c + 3)
             multiply(c)
             if c + 1 < n_chunks:
                 regroup(c + 1)
 
-        nc.sync.dma_start(
-            out=cand_sb[:].rearrange("p (m n) -> p m n", m=ROW_TILES),
-            in_=cand.rearrange("(m p) n -> p m n", p=P),
-        )
         nc.vector.tensor_tensor(out=diff[:], in0=state_sb[:], in1=cand_sb[:], op=ALU.subtract)
 
         sums = [(m, h) for h in range(COL_TILES) for m in range(ROW_TILES)]
@@ -228,18 +244,23 @@ def tile_grulrcell_pb_k_kernel(
             nc.scalar.activation(out=z[:], in_=z[:], func=mybir.ActivationFunctionType.Sigmoid)
             gates[(m, h)] = z
 
-        def blend(m, h):
+        def weigh(m, h):
             cols = slice(m * HIDDEN + h * N_PASS, m * HIDDEN + (h + 1) * N_PASS)
             z = gates[(m, h)]
-            result = work.tile([P, N_PASS], F32, name="result")
             nc.vector.tensor_tensor(out=z[:], in0=z[:], in1=diff[:, cols], op=ALU.mult)
-            nc.vector.tensor_tensor(out=result[:], in0=z[:], in1=cand_sb[:, cols], op=ALU.add)
+
+        def finish(m, h):
+            cols = slice(m * HIDDEN + h * N_PASS, m * HIDDEN + (h + 1) * N_PASS)
+            result = work.tile([P, N_PASS], F32, name="result")
+            nc.vector.tensor_tensor(out=result[:], in0=gates[(m, h)][:], in1=cand_sb[:, cols], op=ALU.add)
             nc.sync.dma_start(
                 out=out[m * P : (m + 1) * P, h * N_PASS : (h + 1) * N_PASS], in_=result[:]
             )
 
-        gate(*sums[0])
-        for i in range(1, len(sums)):
-            gate(*sums[i])
-            blend(*sums[i - 1])
-        blend(*sums[-1])
+        for i in range(len(sums) + 2):
+            if i < len(sums):
+                gate(*sums[i])
+            if 1 <= i <= len(sums):
+                weigh(*sums[i - 1])
+            if i >= 2:
+                finish(*sums[i - 2])

@@ -25,7 +25,6 @@ HALVES = 2
 CHUNK_GROUPS = 4
 QUANT_GROUPS = 2
 SCALE_ROWS = K_PASS // 32
-SET_CHUNKS = 2
 
 FLOPS = 2 * ROWS * (K_INPUT + HIDDEN) * HIDDEN
 
@@ -35,28 +34,21 @@ def tile_grulrcell_pb_k_kernel(
 ):
     nc = tc.nc
 
-    chunks = [dict(rows=state, words=u2_words, first=0, groups=HIDDEN // K_PASS)]
+    chunks = [dict(rows=state, words=u2_words, scales=u2_scales, first=0, groups=HIDDEN // K_PASS)]
     for first in range(0, K_INPUT // K_PASS, CHUNK_GROUPS):
-        chunks.append(dict(rows=inp, words=w2_words, first=first, groups=CHUNK_GROUPS))
+        chunks.append(
+            dict(rows=inp, words=w2_words, scales=w2_scales, first=first, groups=CHUNK_GROUPS)
+        )
     n_chunks = len(chunks)
     total_groups = 0
     for chunk in chunks:
         chunk["plane"] = total_groups
         total_groups += chunk["groups"]
-    set_groups = SET_CHUNKS * CHUNK_GROUPS
-    sets = [dict(scales=u2_scales, first=0, groups=HIDDEN // K_PASS)]
-    for first in range(0, K_INPUT // K_PASS, set_groups):
-        sets.append(dict(scales=w2_scales, first=first, groups=set_groups))
-    chunks[0]["set"] = 0
-    chunks[0]["in_set"] = 0
-    for c in range(1, n_chunks):
-        chunks[c]["set"] = 1 + (c - 1) // SET_CHUNKS
-        chunks[c]["in_set"] = ((c - 1) % SET_CHUNKS) * CHUNK_GROUPS
 
     with ExitStack() as ctx:
         const = ctx.enter_context(tc.tile_pool(name="const", bufs=1))
-        raw_pool = ctx.enter_context(tc.tile_pool(name="raw", bufs=3))
-        sorted_pool = ctx.enter_context(tc.tile_pool(name="sorted", bufs=2))
+        raw_pool = ctx.enter_context(tc.tile_pool(name="raw", bufs=3 * ROW_TILES))
+        sorted_pool = ctx.enter_context(tc.tile_pool(name="sorted", bufs=2 * ROW_TILES))
         grouped_pool = ctx.enter_context(tc.tile_pool(name="grouped", bufs=2))
         codes_pool = ctx.enter_context(tc.tile_pool(name="codes", bufs=3))
         w_pool = ctx.enter_context(tc.tile_pool(name="weights", bufs=4))
@@ -70,9 +62,11 @@ def tile_grulrcell_pb_k_kernel(
         bias_rows = const.tile([P, HIDDEN], BF16)
         bias_all = const.tile([P, HIDDEN], F32)
         table_warm = const.tile([P, 1], F32)
-        state_sb = const.tile([P, ROW_TILES * HIDDEN], BF16)
-        cand_sb = const.tile([P, ROW_TILES * HIDDEN], BF16)
-        diff = const.tile([P, ROW_TILES * HIDDEN], F32)
+        state_sb, cand_sb, diff = {}, {}, {}
+        for m in range(ROW_TILES):
+            state_sb[m] = const.tile([P, HIDDEN], BF16, name="state_sb_%d" % m)
+            cand_sb[m] = const.tile([P, HIDDEN], BF16, name="cand_sb_%d" % m)
+            diff[m] = const.tile([P, HIDDEN], F32, name="diff_%d" % m)
         acc = {}
         for m in range(ROW_TILES):
             for h in range(COL_TILES):
@@ -83,34 +77,29 @@ def tile_grulrcell_pb_k_kernel(
         def load_rows(c):
             chunk = chunks[c]
             k_cols = slice(chunk["first"] * K_PASS, (chunk["first"] + chunk["groups"]) * K_PASS)
-            if c == 0:
-                x_raw = state_sb
-            else:
-                x_raw = raw_pool.tile([P, ROW_TILES * chunk["groups"] * K_PASS], BF16)
-            nc.sync.dma_start(
-                out=x_raw[:].rearrange("p (m k) -> p m k", m=ROW_TILES),
-                in_=chunk["rows"].rearrange("(m p) k -> p m k", p=P)[:, :, k_cols],
-            )
-            raw[c] = x_raw
+            for m in range(ROW_TILES):
+                if c == 0:
+                    x_raw = state_sb[m]
+                else:
+                    x_raw = raw_pool.tile([P, chunk["groups"] * K_PASS], BF16)
+                nc.sync.dma_start(out=x_raw[:], in_=chunk["rows"][m * P : (m + 1) * P, k_cols])
+                raw[(c, m)] = x_raw
 
-        def zero_planes(s):
-            w_planes = const.tile([P, sets[s]["groups"], HIDDEN], U8, align_bytes=64, name="w_planes_%d" % s)
+        def zero_planes(c):
+            w_planes = const.tile([P, chunks[c]["groups"], HIDDEN], U8, align_bytes=64, name="w_planes_%d" % c)
             nc.vector.memset(w_planes[:].bitcast(I32), 0)
-            planes_of[s] = w_planes
+            planes_of[c] = w_planes
 
-        def load_scale_rows(s, rows, apart):
-            groups = slice(sets[s]["first"], sets[s]["first"] + sets[s]["groups"])
-            for q in rows:
-                nc.sync.dma_start(
-                    out=planes_of[s][32 * (q // 4) + q % 4 : P : apart, :, :].bitcast(I32),
-                    in_=sets[s]["scales"]
-                    .bitcast(I32)[groups, q : SCALE_ROWS : apart // 8, :]
-                    .rearrange("g q n -> q g n"),
-                )
-
-        def load_words(c):
+        def load_weights(c):
             chunk = chunks[c]
             groups = slice(chunk["first"], chunk["first"] + chunk["groups"])
+            for r in range(4):
+                nc.sync.dma_start(
+                    out=planes_of[c][r : P : 32, :, :].bitcast(I32),
+                    in_=chunk["scales"]
+                    .bitcast(I32)[groups, r : SCALE_ROWS : 4, :]
+                    .rearrange("g q n -> q g n"),
+                )
             w_words = w_pool.tile([P, chunk["groups"], 2 * HIDDEN], U8, align_bytes=64)
             nc.sync.dma_start(
                 out=w_words[:].bitcast(I32),
@@ -119,26 +108,28 @@ def tile_grulrcell_pb_k_kernel(
             words_of[c] = w_words
 
         def sort_words(c):
-            x_sorted = sorted_pool.tile([P, ROW_TILES * chunks[c]["groups"], HALVES, P], F32)
-            nc.vector.tensor_copy(
-                out=x_sorted[:],
-                in_=raw[c][:].bitcast(F32).rearrange("r (a p u) -> r a u p", p=P, u=HALVES),
-            )
-            sorted_of[c] = x_sorted
+            for m in range(ROW_TILES):
+                x_sorted = sorted_pool.tile([P, chunks[c]["groups"], HALVES, P], F32)
+                nc.vector.tensor_copy(
+                    out=x_sorted[:],
+                    in_=raw[(c, m)][:].bitcast(F32).rearrange("r (g p u) -> r g u p", p=P, u=HALVES),
+                )
+                sorted_of[(c, m)] = x_sorted
 
         def transpose(c):
             n_groups = chunks[c]["groups"]
             banks_of[c] = []
             for g in range(n_groups):
                 xt = xt_pool.tile([P, ROW_TILES, HALVES, P], F32, tag="xt")
-                for m in range(ROW_TILES):
+                banks_of[c].append(xt)
+            for m in range(ROW_TILES):
+                for g in range(n_groups):
                     for u in range(HALVES):
                         nc.tensor.transpose(
-                            out=xt[:, m, u, :],
-                            in_=sorted_of[c][:, m * n_groups + g, u, :],
+                            out=banks_of[c][g][:, m, u, :],
+                            in_=sorted_of[(c, m)][:, g, u, :],
                             identity=ident[:],
                         )
-                banks_of[c].append(xt)
 
         def regroup(c):
             n_groups = chunks[c]["groups"]
@@ -177,9 +168,7 @@ def tile_grulrcell_pb_k_kernel(
                             lhsT=codes_of[c][:, g, m * P : (m + 1) * P].bitcast(FP8X4),
                             lhsT_scale=scales_of[c][:, g, m * P : (m + 1) * P],
                             rhs=words_of[c][:, g, h * 2 * N_PASS : (h + 1) * 2 * N_PASS].bitcast(FP4X4),
-                            rhs_scale=planes_of[chunk["set"]][
-                                :, chunk["in_set"] + g, h * N_PASS : (h + 1) * N_PASS
-                            ],
+                            rhs_scale=planes_of[c][:, g, h * N_PASS : (h + 1) * N_PASS],
                             start=(plane == 0),
                             stop=(plane == total_groups - 1),
                         )
@@ -191,35 +180,29 @@ def tile_grulrcell_pb_k_kernel(
                 nc.tensor.matmul(out=spread[:], lhsT=ones[:], rhs=bias_rows[:, cols], start=True, stop=True)
                 nc.scalar.copy(out=bias_all[:, cols], in_=spread[:])
 
-        nc.vector.memset(bias_rows[:], 0.0)
-        nc.vector.memset(ones[:], 1.0)
-        for s in range(len(sets)):
-            zero_planes(s)
         load_rows(0)
-        load_scale_rows(0, range(4), 32)
         load_rows(1)
+        nc.gpsimd.memset(bias_rows[:], 0.0)
+        nc.gpsimd.memset(ones[:], 1.0)
         nc.scalar.dma_start(out=bias_rows[0:1, :], in_=bias_gate)
         nc.scalar.activation(
             out=table_warm[:], in_=ones[:, 0:1], func=mybir.ActivationFunctionType.Sigmoid
         )
         make_identity(nc, ident[:])
 
+        zero_planes(0)
         sort_words(0)
         transpose(0)
         regroup(0)
         spread_bias()
+        zero_planes(1)
         sort_words(1)
 
-        half_rows = SCALE_ROWS // 4
         for c in range(n_chunks):
-            if 1 + c // 2 < len(sets):
-                load_scale_rows(1 + c // 2, range((c % 2) * half_rows, (c % 2 + 1) * half_rows), 64)
             if c == n_chunks - 1:
-                nc.sync.dma_start(
-                    out=cand_sb[:].rearrange("p (m n) -> p m n", m=ROW_TILES),
-                    in_=cand.rearrange("(m p) n -> p m n", p=P),
-                )
-            load_words(c)
+                for m in range(ROW_TILES):
+                    nc.sync.dma_start(out=cand_sb[m][:], in_=cand[m * P : (m + 1) * P, :])
+            load_weights(c)
             if c + 2 < n_chunks:
                 load_rows(c + 2)
             if c + 1 < n_chunks:
@@ -227,35 +210,34 @@ def tile_grulrcell_pb_k_kernel(
             quantise(c)
             if c + 2 < n_chunks:
                 sort_words(c + 2)
+                zero_planes(c + 2)
             multiply(c)
             if c + 1 < n_chunks:
                 regroup(c + 1)
 
-        nc.vector.tensor_tensor(out=diff[:], in0=state_sb[:], in1=cand_sb[:], op=ALU.subtract)
+        for m in range(ROW_TILES):
+            nc.vector.tensor_tensor(out=diff[m][:], in0=state_sb[m][:], in1=cand_sb[m][:], op=ALU.subtract)
 
         sums = [(m, h) for h in range(COL_TILES) for m in range(ROW_TILES)]
         gates = {}
 
         def gate(m, h):
+            cols = slice(h * N_PASS, (h + 1) * N_PASS)
             z = work.tile([P, N_PASS], F32, name="z")
-            nc.vector.tensor_tensor(
-                out=z[:], in0=acc[(m, h)][:], in1=bias_all[:, h * N_PASS : (h + 1) * N_PASS], op=ALU.add
-            )
+            nc.vector.tensor_tensor(out=z[:], in0=acc[(m, h)][:], in1=bias_all[:, cols], op=ALU.add)
             nc.scalar.activation(out=z[:], in_=z[:], func=mybir.ActivationFunctionType.Sigmoid)
             gates[(m, h)] = z
 
         def weigh(m, h):
-            cols = slice(m * HIDDEN + h * N_PASS, m * HIDDEN + (h + 1) * N_PASS)
+            cols = slice(h * N_PASS, (h + 1) * N_PASS)
             z = gates[(m, h)]
-            nc.vector.tensor_tensor(out=z[:], in0=z[:], in1=diff[:, cols], op=ALU.mult)
+            nc.vector.tensor_tensor(out=z[:], in0=z[:], in1=diff[m][:, cols], op=ALU.mult)
 
         def finish(m, h):
-            cols = slice(m * HIDDEN + h * N_PASS, m * HIDDEN + (h + 1) * N_PASS)
+            cols = slice(h * N_PASS, (h + 1) * N_PASS)
             result = work.tile([P, N_PASS], F32, name="result")
-            nc.vector.tensor_tensor(out=result[:], in0=gates[(m, h)][:], in1=cand_sb[:, cols], op=ALU.add)
-            nc.sync.dma_start(
-                out=out[m * P : (m + 1) * P, h * N_PASS : (h + 1) * N_PASS], in_=result[:]
-            )
+            nc.vector.tensor_tensor(out=result[:], in0=gates[(m, h)][:], in1=cand_sb[m][:, cols], op=ALU.add)
+            nc.sync.dma_start(out=out[m * P : (m + 1) * P, cols], in_=result[:])
 
         for i in range(len(sums) + 2):
             if i < len(sums):

@@ -35,9 +35,11 @@ def tile_grulrcell_pb_k_kernel(
     nc = tc.nc
 
     chunks = [dict(rows=state, words=u2_words, scales=u2_scales, first=0, groups=HIDDEN // K_PASS)]
-    for first in range(0, K_INPUT // K_PASS, CHUNK_GROUPS):
+    half = CHUNK_GROUPS // 2
+    firsts = [0] + list(range(half, K_INPUT // K_PASS, CHUNK_GROUPS))
+    for first, end in zip(firsts, firsts[1:] + [K_INPUT // K_PASS]):
         chunks.append(
-            dict(rows=inp, words=w2_words, scales=w2_scales, first=first, groups=CHUNK_GROUPS)
+            dict(rows=inp, words=w2_words, scales=w2_scales, first=first, groups=end - first)
         )
     n_chunks = len(chunks)
     total_groups = 0
@@ -157,21 +159,19 @@ def tile_grulrcell_pb_k_kernel(
             codes_of[c] = x_codes
             scales_of[c] = x_scales
 
-        def multiply(c):
+        def multiply(c, m, h):
             chunk = chunks[c]
-            for h in range(COL_TILES):
-                for m in range(ROW_TILES):
-                    for g in range(chunk["groups"]):
-                        plane = chunk["plane"] + g
-                        nc.tensor.matmul_mx(
-                            out=acc[(m, h)][:],
-                            lhsT=codes_of[c][:, g, m * P : (m + 1) * P].bitcast(FP8X4),
-                            lhsT_scale=scales_of[c][:, g, m * P : (m + 1) * P],
-                            rhs=words_of[c][:, g, h * 2 * N_PASS : (h + 1) * 2 * N_PASS].bitcast(FP4X4),
-                            rhs_scale=planes_of[c][:, g, h * N_PASS : (h + 1) * N_PASS],
-                            start=(plane == 0),
-                            stop=(plane == total_groups - 1),
-                        )
+            for g in range(chunk["groups"]):
+                plane = chunk["plane"] + g
+                nc.tensor.matmul_mx(
+                    out=acc[(m, h)][:],
+                    lhsT=codes_of[c][:, g, m * P : (m + 1) * P].bitcast(FP8X4),
+                    lhsT_scale=scales_of[c][:, g, m * P : (m + 1) * P],
+                    rhs=words_of[c][:, g, h * 2 * N_PASS : (h + 1) * 2 * N_PASS].bitcast(FP4X4),
+                    rhs_scale=planes_of[c][:, g, h * N_PASS : (h + 1) * N_PASS],
+                    start=(plane == 0),
+                    stop=(plane == total_groups - 1),
+                )
 
         def spread_bias():
             for h in range(COL_TILES):
@@ -182,7 +182,7 @@ def tile_grulrcell_pb_k_kernel(
 
         load_rows(0)
         load_rows(1)
-        nc.gpsimd.memset(bias_rows[:], 0.0)
+        nc.vector.memset(bias_rows[:], 0.0)
         nc.gpsimd.memset(ones[:], 1.0)
         nc.scalar.dma_start(out=bias_rows[0:1, :], in_=bias_gate)
         nc.scalar.activation(
@@ -194,55 +194,69 @@ def tile_grulrcell_pb_k_kernel(
         sort_words(0)
         transpose(0)
         regroup(0)
-        spread_bias()
         zero_planes(1)
         sort_words(1)
 
-        for c in range(n_chunks):
-            if c == n_chunks - 1:
+        sums = [(m, h) for h in range(COL_TILES) for m in range(ROW_TILES)]
+
+        for c in range(n_chunks - 2):
+            load_weights(c)
+            load_rows(c + 2)
+            if c == n_chunks - 4:
                 for m in range(ROW_TILES):
                     nc.sync.dma_start(out=cand_sb[m][:], in_=cand[m * P : (m + 1) * P, :])
-            load_weights(c)
-            if c + 2 < n_chunks:
-                load_rows(c + 2)
-            if c + 1 < n_chunks:
-                transpose(c + 1)
+            transpose(c + 1)
             quantise(c)
-            if c + 2 < n_chunks:
-                sort_words(c + 2)
-                zero_planes(c + 2)
-            multiply(c)
-            if c + 1 < n_chunks:
-                regroup(c + 1)
+            sort_words(c + 2)
+            zero_planes(c + 2)
+            for m, h in sums[:-1]:
+                multiply(c, m, h)
+            regroup(c + 1)
+            if c == 0:
+                spread_bias()
+            if c == n_chunks - 3:
+                transpose(c + 2)
+                regroup(c + 2)
+            multiply(c, *sums[-1])
 
+        load_weights(n_chunks - 2)
+        load_weights(n_chunks - 1)
+        quantise(n_chunks - 2)
         for m in range(ROW_TILES):
             nc.vector.tensor_tensor(out=diff[m][:], in0=state_sb[m][:], in1=cand_sb[m][:], op=ALU.subtract)
+        quantise(n_chunks - 1)
+        for m, h in sums:
+            multiply(n_chunks - 2, m, h)
+            multiply(n_chunks - 1, m, h)
 
-        sums = [(m, h) for h in range(COL_TILES) for m in range(ROW_TILES)]
         gates = {}
 
-        def gate(m, h):
-            cols = slice(h * N_PASS, (h + 1) * N_PASS)
-            z = work.tile([P, N_PASS], F32, name="z")
-            nc.vector.tensor_tensor(out=z[:], in0=acc[(m, h)][:], in1=bias_all[:, cols], op=ALU.add)
-            nc.scalar.activation(out=z[:], in_=z[:], func=mybir.ActivationFunctionType.Sigmoid)
-            gates[(m, h)] = z
+        def gate(m, first, width):
+            cols = slice(first, first + width)
+            bank = slice(first % N_PASS, first % N_PASS + width)
+            z = work.tile([P, N_PASS], F32, name="z")[:, 0:width]
+            nc.vector.tensor_tensor(out=z, in0=acc[(m, first // N_PASS)][:, bank], in1=bias_all[:, cols], op=ALU.add)
+            nc.scalar.activation(out=z, in_=z, func=mybir.ActivationFunctionType.Sigmoid)
+            gates[(m, first)] = z
 
-        def weigh(m, h):
-            cols = slice(h * N_PASS, (h + 1) * N_PASS)
-            z = gates[(m, h)]
-            nc.vector.tensor_tensor(out=z[:], in0=z[:], in1=diff[m][:, cols], op=ALU.mult)
+        def weigh(m, first, width):
+            z = gates[(m, first)]
+            nc.vector.tensor_tensor(out=z, in0=z, in1=diff[m][:, first : first + width], op=ALU.mult)
 
-        def finish(m, h):
-            cols = slice(h * N_PASS, (h + 1) * N_PASS)
-            result = work.tile([P, N_PASS], F32, name="result")
-            nc.vector.tensor_tensor(out=result[:], in0=gates[(m, h)][:], in1=cand_sb[m][:, cols], op=ALU.add)
-            nc.sync.dma_start(out=out[m * P : (m + 1) * P, cols], in_=result[:])
+        def finish(m, first, width):
+            cols = slice(first, first + width)
+            result = work.tile([P, N_PASS], F32, name="result")[:, 0:width]
+            nc.vector.tensor_tensor(out=result, in0=gates[(m, first)], in1=cand_sb[m][:, cols], op=ALU.add)
+            nc.sync.dma_start(out=out[m * P : (m + 1) * P, cols], in_=result)
 
-        for i in range(len(sums) + 2):
-            if i < len(sums):
-                gate(*sums[i])
-            if 1 <= i <= len(sums):
-                weigh(*sums[i - 1])
+        parts = [(m, h * N_PASS, N_PASS) for m, h in sums[:-1]]
+        m, h = sums[-1]
+        half_pass = N_PASS // 2
+        parts += [(m, h * N_PASS, half_pass), (m, h * N_PASS + half_pass, half_pass)]
+        for i in range(len(parts) + 2):
+            if i < len(parts):
+                gate(*parts[i])
+            if 1 <= i <= len(parts):
+                weigh(*parts[i - 1])
             if i >= 2:
-                finish(*sums[i - 2])
+                finish(*parts[i - 2])

@@ -25,6 +25,7 @@ HALVES = 2
 CHUNK_GROUPS = 4
 QUANT_GROUPS = 2
 SCALE_ROWS = K_PASS // 32
+LONG_UNIT = 4
 
 FLOPS = 2 * ROWS * (K_INPUT + HIDDEN) * HIDDEN
 
@@ -42,6 +43,7 @@ def tile_grulrcell_pb_k_kernel(
             dict(rows=inp, words=w2_words, scales=w2_scales, first=first, groups=end - first)
         )
     n_chunks = len(chunks)
+    scale_units = [[0], [1], [2, 3], [4, 5, 6, 7], [8, 9]]
     total_groups = 0
     for chunk in chunks:
         chunk["plane"] = total_groups
@@ -69,14 +71,18 @@ def tile_grulrcell_pb_k_kernel(
             state_sb[m] = const.tile([P, HIDDEN], BF16, name="state_sb_%d" % m)
             cand_sb[m] = const.tile([P, HIDDEN], BF16, name="cand_sb_%d" % m)
             diff[m] = const.tile([P, HIDDEN], F32, name="diff_%d" % m)
+        planes = {}
+        for cs in scale_units:
+            groups = sum(chunks[c]["groups"] for c in cs)
+            planes[cs[0]] = const.tile([P, groups, HIDDEN], U8, align_bytes=64, name="planes_%d" % cs[0])
         acc = {}
         for m in range(ROW_TILES):
             for h in range(COL_TILES):
                 acc[(m, h)] = acc_pool.tile([P, N_PASS], F32, name="acc_%d_%d" % (m, h))
 
-        raw, words_of, planes_of, sorted_of, banks_of, grouped_of, codes_of, scales_of = {}, {}, {}, {}, {}, {}, {}, {}
+        raw, words_of, sorted_of, banks_of, grouped_of, codes_of, scales_of = {}, {}, {}, {}, {}, {}, {}
 
-        def load_rows(c):
+        def load_rows(c, scale_dmas=0):
             chunk = chunks[c]
             k_cols = slice(chunk["first"] * K_PASS, (chunk["first"] + chunk["groups"]) * K_PASS)
             for m in range(ROW_TILES):
@@ -86,22 +92,35 @@ def tile_grulrcell_pb_k_kernel(
                     x_raw = raw_pool.tile([P, chunk["groups"] * K_PASS], BF16)
                 nc.sync.dma_start(out=x_raw[:], in_=chunk["rows"][m * P : (m + 1) * P, k_cols])
                 raw[(c, m)] = x_raw
+                load_some_scales(scale_dmas)
 
         def zero_planes(c):
-            w_planes = const.tile([P, chunks[c]["groups"], HIDDEN], U8, align_bytes=64, name="w_planes_%d" % c)
-            nc.vector.memset(w_planes[:].bitcast(I32), 0)
-            planes_of[c] = w_planes
+            nc.vector.memset(planes[c][:].bitcast(I32), 0)
+
+        def scale_dma(c, rows, partitions):
+            first = chunks[c]["first"]
+            nc.sync.dma_start(
+                out=planes[c][partitions, :, :].bitcast(I32),
+                in_=chunks[c]["scales"]
+                .bitcast(I32)[first : first + planes[c].shape[1], rows, :]
+                .rearrange("g q n -> q g n"),
+            )
+
+        def load_scales(c):
+            for r in range(4):
+                scale_dma(c, slice(r, SCALE_ROWS, 4), slice(r, P, 32))
+
+        waiting_rows = [q for i in range(SCALE_ROWS // 2) for q in (i, i + SCALE_ROWS // 2)]
+
+        def load_some_scales(count):
+            for q in waiting_rows[:count]:
+                waiting_rows.remove(q)
+                row = 32 * (q // 4) + q % 4
+                scale_dma(LONG_UNIT, slice(q, q + 1), slice(row, row + 1))
 
         def load_weights(c):
             chunk = chunks[c]
             groups = slice(chunk["first"], chunk["first"] + chunk["groups"])
-            for r in range(4):
-                nc.sync.dma_start(
-                    out=planes_of[c][r : P : 32, :, :].bitcast(I32),
-                    in_=chunk["scales"]
-                    .bitcast(I32)[groups, r : SCALE_ROWS : 4, :]
-                    .rearrange("g q n -> q g n"),
-                )
             w_words = w_pool.tile([P, chunk["groups"], 2 * HIDDEN], U8, align_bytes=64)
             nc.sync.dma_start(
                 out=w_words[:].bitcast(I32),
@@ -159,16 +178,21 @@ def tile_grulrcell_pb_k_kernel(
             codes_of[c] = x_codes
             scales_of[c] = x_scales
 
+        def plane_of(c, g):
+            first = max(cs[0] for cs in scale_units if cs[0] <= c)
+            return planes[first][:, chunks[c]["first"] - chunks[first]["first"] + g, :]
+
         def multiply(c, m, h):
             chunk = chunks[c]
             for g in range(chunk["groups"]):
                 plane = chunk["plane"] + g
+                w_plane = plane_of(c, g)
                 nc.tensor.matmul_mx(
                     out=acc[(m, h)][:],
                     lhsT=codes_of[c][:, g, m * P : (m + 1) * P].bitcast(FP8X4),
                     lhsT_scale=scales_of[c][:, g, m * P : (m + 1) * P],
                     rhs=words_of[c][:, g, h * 2 * N_PASS : (h + 1) * 2 * N_PASS].bitcast(FP4X4),
-                    rhs_scale=planes_of[c][:, g, h * N_PASS : (h + 1) * N_PASS],
+                    rhs_scale=w_plane[:, h * N_PASS : (h + 1) * N_PASS],
                     start=(plane == 0),
                     stop=(plane == total_groups - 1),
                 )
@@ -180,35 +204,44 @@ def tile_grulrcell_pb_k_kernel(
                 nc.tensor.matmul(out=spread[:], lhsT=ones[:], rhs=bias_rows[:, cols], start=True, stop=True)
                 nc.scalar.copy(out=bias_all[:, cols], in_=spread[:])
 
+        for c in (0, 1):
+            zero_planes(c)
         load_rows(0)
         load_rows(1)
-        nc.vector.memset(bias_rows[:], 0.0)
         nc.gpsimd.memset(ones[:], 1.0)
-        nc.scalar.dma_start(out=bias_rows[0:1, :], in_=bias_gate)
         nc.scalar.activation(
             out=table_warm[:], in_=ones[:, 0:1], func=mybir.ActivationFunctionType.Sigmoid
         )
         make_identity(nc, ident[:])
+        nc.gpsimd.memset(bias_rows[:], 0.0)
+        nc.scalar.dma_start(out=bias_rows[0:1, :], in_=bias_gate)
+        for first in range(0, planes[LONG_UNIT].shape[1], 2):
+            nc.gpsimd.memset(planes[LONG_UNIT][:, first : first + 2, :].bitcast(I32), 0)
 
-        zero_planes(0)
         sort_words(0)
         transpose(0)
         regroup(0)
-        zero_planes(1)
+        zero_planes(2)
         sort_words(1)
 
         sums = [(m, h) for h in range(COL_TILES) for m in range(ROW_TILES)]
 
         for c in range(n_chunks - 2):
+            if c in (0, 1):
+                load_scales(c)
             load_weights(c)
-            load_rows(c + 2)
+            if c + 1 in (2, n_chunks - 2):
+                load_scales(c + 1)
+            load_some_scales(0 if c < 2 else 4)
+            load_rows(c + 2, 0 if c < 2 else 2)
             if c == n_chunks - 4:
                 for m in range(ROW_TILES):
                     nc.sync.dma_start(out=cand_sb[m][:], in_=cand[m * P : (m + 1) * P, :])
             transpose(c + 1)
             quantise(c)
             sort_words(c + 2)
-            zero_planes(c + 2)
+            if c == 3:
+                zero_planes(8)
             for m, h in sums[:-1]:
                 multiply(c, m, h)
             regroup(c + 1)

@@ -82,20 +82,19 @@ def tile_grulrcell_pb_k_kernel(
 
         raw, words_of, sorted_of, banks_of, grouped_of, codes_of, scales_of = {}, {}, {}, {}, {}, {}, {}
 
-        def load_rows(c, scale_dmas=0):
+        def load_rows(c, m):
             chunk = chunks[c]
             k_cols = slice(chunk["first"] * K_PASS, (chunk["first"] + chunk["groups"]) * K_PASS)
-            for m in range(ROW_TILES):
-                if c == 0:
-                    x_raw = state_sb[m]
-                else:
-                    x_raw = raw_pool.tile([P, chunk["groups"] * K_PASS], BF16)
-                nc.sync.dma_start(out=x_raw[:], in_=chunk["rows"][m * P : (m + 1) * P, k_cols])
-                raw[(c, m)] = x_raw
-                load_some_scales(scale_dmas)
+            if c == 0:
+                x_raw = state_sb[m]
+            else:
+                x_raw = raw_pool.tile([P, chunk["groups"] * K_PASS], BF16)
+            nc.sync.dma_start(out=x_raw[:], in_=chunk["rows"][m * P : (m + 1) * P, k_cols])
+            raw[(c, m)] = x_raw
 
-        def zero_planes(c):
-            nc.vector.memset(planes[c][:].bitcast(I32), 0)
+        def zero_planes(c, part=0, parts=1):
+            groups = planes[c].shape[1] // parts
+            nc.vector.memset(planes[c][:, part * groups : (part + 1) * groups, :].bitcast(I32), 0)
 
         def scale_dma(c, rows, partitions):
             first = chunks[c]["first"]
@@ -106,8 +105,8 @@ def tile_grulrcell_pb_k_kernel(
                 .rearrange("g q n -> q g n"),
             )
 
-        def load_scales(c):
-            for r in range(4):
+        def load_scales(c, rs=range(4)):
+            for r in rs:
                 scale_dma(c, slice(r, SCALE_ROWS, 4), slice(r, P, 32))
 
         waiting_rows = [q for i in range(SCALE_ROWS // 2) for q in (i, i + SCALE_ROWS // 2)]
@@ -204,10 +203,12 @@ def tile_grulrcell_pb_k_kernel(
                 nc.tensor.matmul(out=spread[:], lhsT=ones[:], rhs=bias_rows[:, cols], start=True, stop=True)
                 nc.scalar.copy(out=bias_all[:, cols], in_=spread[:])
 
-        for c in (0, 1):
+        for c in (0, 1, 2):
             zero_planes(c)
-        load_rows(0)
-        load_rows(1)
+        zero_planes(LONG_UNIT, 0, 2)
+        for c in (0, 1):
+            for m in range(ROW_TILES):
+                load_rows(c, m)
         nc.gpsimd.memset(ones[:], 1.0)
         nc.scalar.activation(
             out=table_warm[:], in_=ones[:, 0:1], func=mybir.ActivationFunctionType.Sigmoid
@@ -215,26 +216,27 @@ def tile_grulrcell_pb_k_kernel(
         make_identity(nc, ident[:])
         nc.gpsimd.memset(bias_rows[:], 0.0)
         nc.scalar.dma_start(out=bias_rows[0:1, :], in_=bias_gate)
-        for first in range(0, planes[LONG_UNIT].shape[1], 2):
-            nc.gpsimd.memset(planes[LONG_UNIT][:, first : first + 2, :].bitcast(I32), 0)
 
         sort_words(0)
         transpose(0)
         regroup(0)
-        zero_planes(2)
+        zero_planes(LONG_UNIT, 1, 2)
         sort_words(1)
 
         sums = [(m, h) for h in range(COL_TILES) for m in range(ROW_TILES)]
 
-        for c in range(n_chunks - 2):
+        closing = range(n_chunks - 3, n_chunks)
+        for c in range(n_chunks - 3):
             if c in (0, 1):
                 load_scales(c)
             load_weights(c)
-            if c + 1 in (2, n_chunks - 2):
-                load_scales(c + 1)
-            load_some_scales(0 if c < 2 else 4)
-            load_rows(c + 2, 0 if c < 2 else 2)
-            if c == n_chunks - 4:
+            for m in range(ROW_TILES):
+                if c in (0, 1):
+                    load_scales(2, (2 * c + m,))
+                load_some_scales(3 if c in (2, 3) else 0)
+                load_rows(c + 2, m)
+            load_some_scales(3 if c in (2, 3) else 0)
+            if c == closing[0] - 2:
                 for m in range(ROW_TILES):
                     nc.sync.dma_start(out=cand_sb[m][:], in_=cand[m * P : (m + 1) * P, :])
             transpose(c + 1)
@@ -242,25 +244,41 @@ def tile_grulrcell_pb_k_kernel(
             sort_words(c + 2)
             if c == 3:
                 zero_planes(8)
+            if c == closing[0] - 1:
+                for m in range(ROW_TILES):
+                    nc.vector.tensor_tensor(
+                        out=diff[m][:], in0=state_sb[m][:], in1=cand_sb[m][:], op=ALU.subtract
+                    )
             for m, h in sums[:-1]:
                 multiply(c, m, h)
             regroup(c + 1)
             if c == 0:
                 spread_bias()
-            if c == n_chunks - 3:
+            if c + 1 == closing[0]:
                 transpose(c + 2)
                 regroup(c + 2)
             multiply(c, *sums[-1])
 
-        load_weights(n_chunks - 2)
-        load_weights(n_chunks - 1)
-        quantise(n_chunks - 2)
+        load_weights(closing[0])
         for m in range(ROW_TILES):
-            nc.vector.tensor_tensor(out=diff[m][:], in0=state_sb[m][:], in1=cand_sb[m][:], op=ALU.subtract)
-        quantise(n_chunks - 1)
+            load_rows(closing[2], m)
+        load_scales(closing[1])
+        load_weights(closing[1])
+        load_weights(closing[2])
+        quantise(closing[0])
+        sort_words(closing[2])
+        quantise(closing[1])
+        early = sums[:2]
+        multiply(closing[0], *early[0])
+        transpose(closing[2])
+        regroup(closing[2])
+        quantise(closing[2])
+        multiply(closing[0], *early[1])
         for m, h in sums:
-            multiply(n_chunks - 2, m, h)
-            multiply(n_chunks - 1, m, h)
+            if (m, h) not in early:
+                multiply(closing[0], m, h)
+            multiply(closing[1], m, h)
+            multiply(closing[2], m, h)
 
         gates = {}
 
@@ -282,14 +300,15 @@ def tile_grulrcell_pb_k_kernel(
             nc.vector.tensor_tensor(out=result, in0=gates[(m, first)], in1=cand_sb[m][:, cols], op=ALU.add)
             nc.sync.dma_start(out=out[m * P : (m + 1) * P, cols], in_=result)
 
-        parts = [(m, h * N_PASS, N_PASS) for m, h in sums[:-1]]
+        for i in range(len(sums) - 1):
+            m, h = sums[i]
+            gate(m, h * N_PASS, N_PASS)
+            if i > 0:
+                finish(sums[i - 1][0], sums[i - 1][1] * N_PASS, N_PASS)
+            weigh(m, h * N_PASS, N_PASS)
+        finish(m, h * N_PASS, N_PASS)
         m, h = sums[-1]
-        half_pass = N_PASS // 2
-        parts += [(m, h * N_PASS, half_pass), (m, h * N_PASS + half_pass, half_pass)]
-        for i in range(len(parts) + 2):
-            if i < len(parts):
-                gate(*parts[i])
-            if 1 <= i <= len(parts):
-                weigh(*parts[i - 1])
-            if i >= 2:
-                finish(*parts[i - 2])
+        halves = [(m, h * N_PASS, N_PASS // 2), (m, h * N_PASS + N_PASS // 2, N_PASS // 2)]
+        for step in (gate, weigh, finish):
+            for half in halves:
+                step(*half)

@@ -74,7 +74,7 @@ def tile_grulrcell_pb_k_kernel(
         planes = {}
         for cs in scale_units:
             groups = sum(chunks[c]["groups"] for c in cs)
-            planes[cs[0]] = const.tile([P, groups, HIDDEN], U8, align_bytes=64, name="planes_%d" % cs[0])
+            planes[cs[0]] = const.tile([P, groups, HIDDEN], U8, align_bytes=256, name="planes_%d" % cs[0])
         acc = {}
         for m in range(ROW_TILES):
             for h in range(COL_TILES):
@@ -120,7 +120,7 @@ def tile_grulrcell_pb_k_kernel(
         def load_weights(c):
             chunk = chunks[c]
             groups = slice(chunk["first"], chunk["first"] + chunk["groups"])
-            w_words = w_pool.tile([P, chunk["groups"], 2 * HIDDEN], U8, align_bytes=64)
+            w_words = w_pool.tile([P, chunk["groups"], 2 * HIDDEN], U8, align_bytes=256)
             nc.sync.dma_start(
                 out=w_words[:].bitcast(I32),
                 in_=chunk["words"].bitcast(I32)[groups].rearrange("g p b -> p g b"),
@@ -153,7 +153,7 @@ def tile_grulrcell_pb_k_kernel(
 
         def regroup(c):
             n_groups = chunks[c]["groups"]
-            grouped = grouped_pool.tile([P, n_groups, ROWS * PACK], BF16, align_bytes=64)
+            grouped = grouped_pool.tile([P, n_groups, ROWS * PACK], BF16, align_bytes=256)
             for g in range(n_groups):
                 nc.scalar.copy(
                     out=grouped[:, g, :]
@@ -165,8 +165,8 @@ def tile_grulrcell_pb_k_kernel(
 
         def quantise(c):
             n_groups = chunks[c]["groups"]
-            x_codes = codes_pool.tile([P, n_groups, ROWS], U32, align_bytes=64)
-            x_scales = codes_pool.tile([P, n_groups, ROWS], U8, align_bytes=64)
+            x_codes = codes_pool.tile([P, n_groups, ROWS], U32, align_bytes=256)
+            x_scales = codes_pool.tile([P, n_groups, ROWS], U8, align_bytes=256)
             for g in range(0, n_groups, QUANT_GROUPS):
                 pair = slice(g, g + QUANT_GROUPS)
                 nc.vector.quantize_mx(

@@ -61,16 +61,16 @@ def tile_grulrcell_pb_k_kernel(
         xt_pool = ctx.enter_context(tc.psum_pool(name="xt", bufs=CHUNK_GROUPS))
         ctx.enter_context(tc.manual_schedule())
 
-        ident = const.tile([P, P], F32)
-        ones = const.tile([P, P], BF16)
-        bias_rows = const.tile([P, HIDDEN], BF16)
-        bias_all = const.tile([P, HIDDEN], F32)
-        table_warm = const.tile([P, 1], F32)
+        ident = const.tile([P, P], F32, align_bytes=256)
+        ones = const.tile([P, P], BF16, align_bytes=256)
+        bias_rows = const.tile([P, HIDDEN], BF16, align_bytes=256)
+        bias_all = const.tile([P, HIDDEN], F32, align_bytes=256)
+        table_warm = const.tile([P, 1], F32, align_bytes=256)
         state_sb, cand_sb, diff = {}, {}, {}
         for m in range(ROW_TILES):
-            state_sb[m] = const.tile([P, HIDDEN], BF16, name="state_sb_%d" % m)
-            cand_sb[m] = const.tile([P, HIDDEN], BF16, name="cand_sb_%d" % m)
-            diff[m] = const.tile([P, HIDDEN], F32, name="diff_%d" % m)
+            state_sb[m] = const.tile([P, HIDDEN], BF16, align_bytes=256, name="state_sb_%d" % m)
+            cand_sb[m] = const.tile([P, HIDDEN], BF16, align_bytes=256, name="cand_sb_%d" % m)
+            diff[m] = const.tile([P, HIDDEN], F32, align_bytes=256, name="diff_%d" % m)
         planes = {}
         for cs in scale_units:
             groups = sum(chunks[c]["groups"] for c in cs)
@@ -88,7 +88,7 @@ def tile_grulrcell_pb_k_kernel(
             if c == 0:
                 x_raw = state_sb[m]
             else:
-                x_raw = raw_pool.tile([P, chunk["groups"] * K_PASS], BF16)
+                x_raw = raw_pool.tile([P, chunk["groups"] * K_PASS], BF16, align_bytes=256)
             nc.sync.dma_start(out=x_raw[:], in_=chunk["rows"][m * P : (m + 1) * P, k_cols])
             raw[(c, m)] = x_raw
 
@@ -129,7 +129,7 @@ def tile_grulrcell_pb_k_kernel(
 
         def sort_words(c):
             for m in range(ROW_TILES):
-                x_sorted = sorted_pool.tile([P, chunks[c]["groups"], HALVES, P], F32)
+                x_sorted = sorted_pool.tile([P, chunks[c]["groups"], HALVES, P], F32, align_bytes=256)
                 nc.vector.tensor_copy(
                     out=x_sorted[:],
                     in_=raw[(c, m)][:].bitcast(F32).rearrange("r (g p u) -> r g u p", p=P, u=HALVES),
@@ -181,20 +181,26 @@ def tile_grulrcell_pb_k_kernel(
             first = max(cs[0] for cs in scale_units if cs[0] <= c)
             return planes[first][:, chunks[c]["first"] - chunks[first]["first"] + g, :]
 
+        def one_pass(c, g, m, h):
+            plane = chunks[c]["plane"] + g
+            nc.tensor.matmul_mx(
+                out=acc[(m, h)][:],
+                lhsT=codes_of[c][:, g, m * P : (m + 1) * P].bitcast(FP8X4),
+                lhsT_scale=scales_of[c][:, g, m * P : (m + 1) * P],
+                rhs=words_of[c][:, g, h * 2 * N_PASS : (h + 1) * 2 * N_PASS].bitcast(FP4X4),
+                rhs_scale=plane_of(c, g)[:, h * N_PASS : (h + 1) * N_PASS],
+                start=(plane == 0),
+                stop=(plane == total_groups - 1),
+            )
+
         def multiply(c, m, h):
-            chunk = chunks[c]
-            for g in range(chunk["groups"]):
-                plane = chunk["plane"] + g
-                w_plane = plane_of(c, g)
-                nc.tensor.matmul_mx(
-                    out=acc[(m, h)][:],
-                    lhsT=codes_of[c][:, g, m * P : (m + 1) * P].bitcast(FP8X4),
-                    lhsT_scale=scales_of[c][:, g, m * P : (m + 1) * P],
-                    rhs=words_of[c][:, g, h * 2 * N_PASS : (h + 1) * 2 * N_PASS].bitcast(FP4X4),
-                    rhs_scale=w_plane[:, h * N_PASS : (h + 1) * N_PASS],
-                    start=(plane == 0),
-                    stop=(plane == total_groups - 1),
-                )
+            for g in range(chunks[c]["groups"]):
+                one_pass(c, g, m, h)
+
+        def multiply_group(c, g):
+            for m in range(ROW_TILES):
+                for h in range(COL_TILES):
+                    one_pass(c, g, m, h)
 
         def spread_bias():
             for h in range(COL_TILES):
@@ -249,15 +255,15 @@ def tile_grulrcell_pb_k_kernel(
                     nc.vector.tensor_tensor(
                         out=diff[m][:], in0=state_sb[m][:], in1=cand_sb[m][:], op=ALU.subtract
                     )
-            for m, h in sums[:-1]:
-                multiply(c, m, h)
+            for g in range(chunks[c]["groups"] - 1):
+                multiply_group(c, g)
             regroup(c + 1)
             if c == 0:
                 spread_bias()
             if c + 1 == closing[0]:
                 transpose(c + 2)
                 regroup(c + 2)
-            multiply(c, *sums[-1])
+            multiply_group(c, chunks[c]["groups"] - 1)
 
         load_weights(closing[0])
         for m in range(ROW_TILES):
@@ -285,7 +291,7 @@ def tile_grulrcell_pb_k_kernel(
         def gate(m, first, width):
             cols = slice(first, first + width)
             bank = slice(first % N_PASS, first % N_PASS + width)
-            z = work.tile([P, N_PASS], F32, name="z")[:, 0:width]
+            z = work.tile([P, N_PASS], F32, align_bytes=256, name="z")[:, 0:width]
             nc.vector.tensor_tensor(out=z, in0=acc[(m, first // N_PASS)][:, bank], in1=bias_all[:, cols], op=ALU.add)
             nc.scalar.activation(out=z, in_=z, func=mybir.ActivationFunctionType.Sigmoid)
             gates[(m, first)] = z
@@ -296,7 +302,7 @@ def tile_grulrcell_pb_k_kernel(
 
         def finish(m, first, width):
             cols = slice(first, first + width)
-            result = work.tile([P, N_PASS], F32, name="result")[:, 0:width]
+            result = work.tile([P, N_PASS], F32, align_bytes=256, name="result")[:, 0:width]
             nc.vector.tensor_tensor(out=result, in0=gates[(m, first)], in1=cand_sb[m][:, cols], op=ALU.add)
             nc.sync.dma_start(out=out[m * P : (m + 1) * P, cols], in_=result)
 

from contextlib import ExitStack

import concourse.mybir as mybir
from concourse.masks import make_identity

BF16 = mybir.dt.bfloat16
F32 = mybir.dt.float32
I32 = mybir.dt.int32
U32 = mybir.dt.uint32
U8 = mybir.dt.uint8
FP8X4 = mybir.dt.float8_e4m3fn_x4
FP4X4 = mybir.dt.float4_e2m1fn_x4
ALU = mybir.AluOpType

P = 128
PACK = 4
K_PASS = P * PACK
ROWS = 256
K_INPUT = 16384
HIDDEN = 1024
ROW_TILES = ROWS // P
N_PASS = 512
COL_TILES = HIDDEN // N_PASS
HALVES = 2
CHUNK_GROUPS = 4
QUANT_GROUPS = 2
SCALE_ROWS = K_PASS // 32
LONG_UNIT = 4

FLOPS = 2 * ROWS * (K_INPUT + HIDDEN) * HIDDEN


def tile_grulrcell_pb_k_kernel(
    tc, inp, state, cand, w2_words, w2_scales, u2_words, u2_scales, bias_gate, out
):
    nc = tc.nc

    chunks = [dict(rows=state, words=u2_words, scales=u2_scales, first=0, groups=HIDDEN // K_PASS)]
    half = CHUNK_GROUPS // 2
    firsts = [0] + list(range(half, K_INPUT // K_PASS, CHUNK_GROUPS))
    for first, end in zip(firsts, firsts[1:] + [K_INPUT // K_PASS]):
        chunks.append(
            dict(rows=inp, words=w2_words, scales=w2_scales, first=first, groups=end - first)
        )
    n_chunks = len(chunks)
    scale_units = [[0], [1], [2, 3], [4, 5, 6, 7], [8, 9]]
    total_groups = 0
    for chunk in chunks:
        chunk["plane"] = total_groups
        total_groups += chunk["groups"]

    with ExitStack() as ctx:
        const = ctx.enter_context(tc.tile_pool(name="const", bufs=1))
        raw_pool = ctx.enter_context(tc.tile_pool(name="raw", bufs=3 * ROW_TILES))
        sorted_pool = ctx.enter_context(tc.tile_pool(name="sorted", bufs=2 * ROW_TILES))
        grouped_pool = ctx.enter_context(tc.tile_pool(name="grouped", bufs=2))
        codes_pool = ctx.enter_context(tc.tile_pool(name="codes", bufs=3))
        w_pool = ctx.enter_context(tc.tile_pool(name="weights", bufs=4))
        work = ctx.enter_context(tc.tile_pool(name="work", bufs=4))
        acc_pool = ctx.enter_context(tc.psum_pool(name="acc", bufs=1))
        xt_pool = ctx.enter_context(tc.psum_pool(name="xt", bufs=CHUNK_GROUPS))
        ctx.enter_context(tc.manual_schedule())

        ident = const.tile([P, P], F32, align_bytes=256)
        ones = const.tile([P, P], BF16, align_bytes=256)
        bias_rows = const.tile([P, HIDDEN], BF16, align_bytes=256)
        bias_all = const.tile([P, HIDDEN], F32, align_bytes=256)
        table_warm = const.tile([P, 1], F32, align_bytes=256)
        state_sb, cand_sb, diff = {}, {}, {}
        for m in range(ROW_TILES):
            state_sb[m] = const.tile([P, HIDDEN], BF16, align_bytes=256, name="state_sb_%d" % m)
            cand_sb[m] = const.tile([P, HIDDEN], BF16, align_bytes=256, name="cand_sb_%d" % m)
            diff[m] = const.tile([P, HIDDEN], F32, align_bytes=256, name="diff_%d" % m)
        planes = {}
        for cs in scale_units:
            groups = sum(chunks[c]["groups"] for c in cs)
            planes[cs[0]] = const.tile([P, groups, HIDDEN], U8, align_bytes=256, name="planes_%d" % cs[0])
        acc = {}
        for m in range(ROW_TILES):
            for h in range(COL_TILES):
                acc[(m, h)] = acc_pool.tile([P, N_PASS], F32, name="acc_%d_%d" % (m, h))

        raw, words_of, sorted_of, banks_of, grouped_of, codes_of, scales_of = {}, {}, {}, {}, {}, {}, {}

        def load_rows(c, m):
            chunk = chunks[c]
            k_cols = slice(chunk["first"] * K_PASS, (chunk["first"] + chunk["groups"]) * K_PASS)
            if c == 0:
                x_raw = state_sb[m]
            else:
                x_raw = raw_pool.tile([P, chunk["groups"] * K_PASS], BF16, align_bytes=256)
            nc.sync.dma_start(out=x_raw[:], in_=chunk["rows"][m * P : (m + 1) * P, k_cols])
            raw[(c, m)] = x_raw

        def zero_planes(c, part=0, parts=1):
            groups = planes[c].shape[1] // parts
            nc.vector.memset(planes[c][:, part * groups : (part + 1) * groups, :].bitcast(I32), 0)

        def scale_dma(c, rows, partitions):
            first = chunks[c]["first"]
            nc.sync.dma_start(
                out=planes[c][partitions, :, :].bitcast(I32),
                in_=chunks[c]["scales"]
                .bitcast(I32)[first : first + planes[c].shape[1], rows, :]
                .rearrange("g q n -> q g n"),
            )

        def load_scales(c, rs=range(4)):
            for r in rs:
                scale_dma(c, slice(r, SCALE_ROWS, 4), slice(r, P, 32))

        waiting_rows = [q for i in range(SCALE_ROWS // 2) for q in (i, i + SCALE_ROWS // 2)]

        def load_some_scales(count):
            for q in waiting_rows[:count]:
                waiting_rows.remove(q)
                row = 32 * (q // 4) + q % 4
                scale_dma(LONG_UNIT, slice(q, q + 1), slice(row, row + 1))

        def load_weights(c):
            chunk = chunks[c]
            groups = slice(chunk["first"], chunk["first"] + chunk["groups"])
            w_words = w_pool.tile([P, chunk["groups"], 2 * HIDDEN], U8, align_bytes=256)
            nc.sync.dma_start(
                out=w_words[:].bitcast(I32),
                in_=chunk["words"].bitcast(I32)[groups].rearrange("g p b -> p g b"),
            )
            words_of[c] = w_words

        def sort_words(c):
            for m in range(ROW_TILES):
                x_sorted = sorted_pool.tile([P, chunks[c]["groups"], HALVES, P], F32, align_bytes=256)
                nc.vector.tensor_copy(
                    out=x_sorted[:],
                    in_=raw[(c, m)][:].bitcast(F32).rearrange("r (g p u) -> r g u p", p=P, u=HALVES),
                )
                sorted_of[(c, m)] = x_sorted

        def transpose(c):
            n_groups = chunks[c]["groups"]
            banks_of[c] = []
            for g in range(n_groups):
                xt = xt_pool.tile([P, ROW_TILES, HALVES, P], F32, tag="xt")
                banks_of[c].append(xt)
            for m in range(ROW_TILES):
                for g in range(n_groups):
                    for u in range(HALVES):
                        nc.tensor.transpose(
                            out=banks_of[c][g][:, m, u, :],
                            in_=sorted_of[(c, m)][:, g, u, :],
                            identity=ident[:],
                        )

        def regroup(c):
            n_groups = chunks[c]["groups"]
            grouped = grouped_pool.tile([P, n_groups, ROWS * PACK], BF16, align_bytes=256)
            for g in range(n_groups):
                nc.scalar.copy(
                    out=grouped[:, g, :]
                    .bitcast(F32)
                    .rearrange("p (m r u) -> p m r u", m=ROW_TILES, u=HALVES),
                    in_=banks_of[c][g][:].rearrange("p m u r -> p m r u"),
                )
            grouped_of[c] = grouped

        def quantise(c):
            n_groups = chunks[c]["groups"]
            x_codes = codes_pool.tile([P, n_groups, ROWS], U32, align_bytes=256)
            x_scales = codes_pool.tile([P, n_groups, ROWS], U8, align_bytes=256)
            for g in range(0, n_groups, QUANT_GROUPS):
                pair = slice(g, g + QUANT_GROUPS)
                nc.vector.quantize_mx(
                    out=x_codes[:, pair, :].rearrange("p g r -> p (g r)").bitcast(FP8X4),
                    scales=x_scales[:, pair, :].rearrange("p g r -> p (g r)"),
                    in_=grouped_of[c][:, pair, :].rearrange("p g f -> p (g f)"),
                )
            codes_of[c] = x_codes
            scales_of[c] = x_scales

        def plane_of(c, g):
            first = max(cs[0] for cs in scale_units if cs[0] <= c)
            return planes[first][:, chunks[c]["first"] - chunks[first]["first"] + g, :]

        def one_pass(c, g, m, h):
            plane = chunks[c]["plane"] + g
            nc.tensor.matmul_mx(
                out=acc[(m, h)][:],
                lhsT=codes_of[c][:, g, m * P : (m + 1) * P].bitcast(FP8X4),
                lhsT_scale=scales_of[c][:, g, m * P : (m + 1) * P],
                rhs=words_of[c][:, g, h * 2 * N_PASS : (h + 1) * 2 * N_PASS].bitcast(FP4X4),
                rhs_scale=plane_of(c, g)[:, h * N_PASS : (h + 1) * N_PASS],
                start=(plane == 0),
                stop=(plane == total_groups - 1),
            )

        def multiply(c, m, h):
            for g in range(chunks[c]["groups"]):
                one_pass(c, g, m, h)

        def multiply_group(c, g):
            for m in range(ROW_TILES):
                for h in range(COL_TILES):
                    one_pass(c, g, m, h)

        def spread_bias():
            for h in range(COL_TILES):
                cols = slice(h * N_PASS, (h + 1) * N_PASS)
                spread = xt_pool.tile([P, N_PASS], F32, tag="xt")
                nc.tensor.matmul(out=spread[:], lhsT=ones[:], rhs=bias_rows[:, cols], start=True, stop=True)
                nc.scalar.copy(out=bias_all[:, cols], in_=spread[:])

        for c in (0, 1, 2):
            zero_planes(c)
        zero_planes(LONG_UNIT, 0, 2)
        for c in (0, 1):
            for m in range(ROW_TILES):
                load_rows(c, m)
        nc.gpsimd.memset(ones[:], 1.0)
        nc.scalar.activation(
            out=table_warm[:], in_=ones[:, 0:1], func=mybir.ActivationFunctionType.Sigmoid
        )
        make_identity(nc, ident[:])
        nc.gpsimd.memset(bias_rows[:], 0.0)
        nc.scalar.dma_start(out=bias_rows[0:1, :], in_=bias_gate)

        sort_words(0)
        transpose(0)
        regroup(0)
        zero_planes(LONG_UNIT, 1, 2)
        sort_words(1)

        sums = [(m, h) for h in range(COL_TILES) for m in range(ROW_TILES)]

        closing = range(n_chunks - 3, n_chunks)
        for c in range(n_chunks - 3):
            if c in (0, 1):
                load_scales(c)
            load_weights(c)
            for m in range(ROW_TILES):
                if c in (0, 1):
                    load_scales(2, (2 * c + m,))
                load_some_scales(3 if c in (2, 3) else 0)
                load_rows(c + 2, m)
            load_some_scales(3 if c in (2, 3) else 0)
            if c == closing[0] - 2:
                for m in range(ROW_TILES):
                    nc.sync.dma_start(out=cand_sb[m][:], in_=cand[m * P : (m + 1) * P, :])
            transpose(c + 1)
            quantise(c)
            sort_words(c + 2)
            if c == 3:
                zero_planes(8)
            if c == closing[0] - 1:
                for m in range(ROW_TILES):
                    nc.vector.tensor_tensor(
                        out=diff[m][:], in0=state_sb[m][:], in1=cand_sb[m][:], op=ALU.subtract
                    )
            for g in range(chunks[c]["groups"] - 1):
                multiply_group(c, g)
            regroup(c + 1)
            if c == 0:
                spread_bias()
            if c + 1 == closing[0]:
                transpose(c + 2)
                regroup(c + 2)
            multiply_group(c, chunks[c]["groups"] - 1)

        load_weights(closing[0])
        for m in range(ROW_TILES):
            load_rows(closing[2], m)
        load_scales(closing[1])
        load_weights(closing[1])
        load_weights(closing[2])
        quantise(closing[0])
        sort_words(closing[2])
        quantise(closing[1])
        early = sums[:2]
        multiply(closing[0], *early[0])
        transpose(closing[2])
        regroup(closing[2])
        quantise(closing[2])
        multiply(closing[0], *early[1])
        for m, h in sums:
            if (m, h) not in early:
                multiply(closing[0], m, h)
            multiply(closing[1], m, h)
            multiply(closing[2], m, h)

        gates = {}

        def gate(m, first, width):
            cols = slice(first, first + width)
            bank = slice(first % N_PASS, first % N_PASS + width)
            z = work.tile([P, N_PASS], F32, align_bytes=256, name="z")[:, 0:width]
            nc.vector.tensor_tensor(out=z, in0=acc[(m, first // N_PASS)][:, bank], in1=bias_all[:, cols], op=ALU.add)
            nc.scalar.activation(out=z, in_=z, func=mybir.ActivationFunctionType.Sigmoid)
            gates[(m, first)] = z

        def weigh(m, first, width):
            z = gates[(m, first)]
            nc.vector.tensor_tensor(out=z, in0=z, in1=diff[m][:, first : first + width], op=ALU.mult)

        def finish(m, first, width):
            cols = slice(first, first + width)
            result = work.tile([P, N_PASS], F32, align_bytes=256, name="result")[:, 0:width]
            nc.vector.tensor_tensor(out=result, in0=gates[(m, first)], in1=cand_sb[m][:, cols], op=ALU.add)
            nc.sync.dma_start(out=out[m * P : (m + 1) * P, cols], in_=result)

        for i in range(len(sums) - 1):
            m, h = sums[i]
            gate(m, h * N_PASS, N_PASS)
            if i > 0:
                finish(sums[i - 1][0], sums[i - 1][1] * N_PASS, N_PASS)
            weigh(m, h * N_PASS, N_PASS)
        finish(m, h * N_PASS, N_PASS)
        m, h = sums[-1]
        halves = [(m, h * N_PASS, N_PASS // 2), (m, h * N_PASS + N_PASS // 2, N_PASS // 2)]
        for step in (gate, weigh, finish):
            for half in halves:
                step(*half)
